import numpy as np
import ml_dtypes


def mxq(x, axis, fmt="e4m3"):
    dtype, down = {"e4m3": (ml_dtypes.float8_e4m3fn, 7), "e5m2": (ml_dtypes.float8_e5m2, 14)}[fmt]
    v = np.moveaxis(np.asarray(x, np.float32).astype(ml_dtypes.bfloat16).astype(np.float64), axis, -1)
    blocks = v.reshape(v.shape[:-1] + (-1, 32))
    amax = np.abs(blocks).max(-1, keepdims=True)
    byte = np.maximum(np.where(amax > 0, np.frexp(amax)[1] - 1 + 127, 0) - down, 1)
    scale = np.exp2(byte - 127.0)
    codes = (blocks / scale).astype(np.float32).astype(dtype).astype(np.float64)
    return np.moveaxis((codes * scale).reshape(v.shape), -1, axis)


WIDE = False


def mx_kscale(k):
    if not WIDE:
        return np.ones(k)
    levels = np.array([10, -10, 5, -5, 0])
    a = np.random.permutation(np.resize(levels, k // 512 * 4)).reshape(k // 512, 4)
    idx = np.arange(k)
    return np.exp2(a[idx // 512, idx % 128 // 32])


BF16 = ml_dtypes.bfloat16


def bf(x):
    return np.asarray(x, np.float32).astype(BF16)


def f64(x):
    return np.asarray(x).astype(np.float64)


B, C, H, W, K, R = 4, 512, 64, 64, 128, 8
EPS = 1e-8


def setup_inputs():
    s = mx_kscale(C)
    core = np.random.standard_normal((R, C)) / np.sqrt(R)
    fa = np.random.standard_normal((B, R, H, W))
    pa = np.random.standard_normal((K, R))
    features = 0.5 * np.random.standard_normal((B, C, H, W))
    prototypes = 0.5 * np.random.standard_normal((K, C))
    for r in range(R):
        features += core[r][None, :, None, None] * fa[:, r][:, None]
        prototypes += pa[:, r][:, None] * core[r][None, :]
    t = s[np.random.randint(0, C, (B, 1, H, W))]
    u = s[np.random.randint(0, C, (K, 1))]
    return {"features": bf(features * t), "prototypes": bf(prototypes * 0.5 / np.sqrt(C) * u)}


def reference(features, prototypes):
    f = f64(features).reshape(B, C, H * W).transpose(0, 2, 1)
    p = f64(prototypes)
    dots = mxq(f, 2, "e4m3") @ mxq(p, 1, "e4m3").T
    f_norm = np.linalg.norm(f, axis=-1)
    p_norm = np.linalg.norm(p, axis=-1)
    denom = np.maximum(f_norm[:, :, None] * p_norm[None, None, :], EPS)
    sim = dots / denom
    return sim.transpose(0, 2, 1).reshape(B, -1, H, W)

@@ -1,0 +1,186 @@
+from contextlib import ExitStack
+
+import concourse.mybir as mybir
+from concourse.masks import make_identity
+
+F32 = mybir.dt.float32
+BF16 = mybir.dt.bfloat16
+U32 = mybir.dt.uint32
+U8 = mybir.dt.uint8
+FP8X4 = mybir.dt.float8_e4m3fn_x4
+ACT = mybir.ActivationFunctionType
+ALU = mybir.AluOpType
+
+P = 128
+PACK = 4
+B, C, HW, K = 4, 512, 4096, 128
+UNIT = 1024
+CHUNK = 512
+GROUP = 256
+N_UNITS = B * HW // UNIT
+EPS = 1e-8
+TINY = 2.0 ** -116
+
+FLOPS = 2 * B * HW * C * K
+
+
+def tile_globalprototype_kernel(tc, features, prototypes, out):
+    nc = tc.nc
+    with ExitStack() as ctx:
+        const = ctx.enter_context(tc.tile_pool(name="const", bufs=1))
+        rawp = ctx.enter_context(tc.tile_pool(name="rawp", bufs=N_UNITS))
+        grpp = ctx.enter_context(tc.tile_pool(name="grpp", bufs=2))
+        codp = ctx.enter_context(tc.tile_pool(name="codp", bufs=3))
+        small = ctx.enter_context(tc.tile_pool(name="small", bufs=4))
+        junkp = ctx.enter_context(tc.tile_pool(name="junkp", bufs=2))
+        wp = ctx.enter_context(tc.tile_pool(name="wp", bufs=4))
+        op = ctx.enter_context(tc.tile_pool(name="op", bufs=3))
+        tps = ctx.enter_context(tc.psum_pool(name="tps", bufs=4))
+        rps = ctx.enter_context(tc.psum_pool(name="rps", bufs=2))
+        dps = ctx.enter_context(tc.psum_pool(name="dps", bufs=2))
+
+        p_sb = const.tile([P, C], BF16)
+        nc.scalar.dma_start(out=p_sb[:], in_=prototypes)
+        raws = []
+        for u in range(N_UNITS):
+            b, off = divmod(u * UNIT, HW)
+            raw = rawp.tile([P, PACK, UNIT], BF16, name="raw")
+            src = features[b].rearrange("(p j) h w -> p j (h w)", j=PACK)
+            nc.sync.dma_start(out=raw[:], in_=src[:, :, off:off + UNIT])
+            raws.append(raw)
+
+        warm = const.tile([P, 1], F32)
+        nc.vector.memset(warm[:], 1.0)
+        nc.scalar.activation(out=warm[:], in_=warm[:], func=ACT.Sqrt)
+        ident_f = const.tile([P, P], F32)
+        make_identity(nc, ident_f[:])
+        ident_b = const.tile([P, P], BF16)
+        make_identity(nc, ident_b[:])
+
+        pjunk = junkp.tile([P, C], BF16, name="junk")
+        pn2 = const.tile([P, 1], F32)
+        nc.scalar.activation(out=pjunk[:], in_=p_sb[:], func=ACT.Square, accum_out=pn2[:])
+        pn2c = const.tile([P, 1], F32)
+        nc.vector.tensor_scalar(out=pn2c[:], in0=pn2[:], scalar1=TINY, scalar2=None, op0=ALU.max)
+        pinv = const.tile([P, 1], F32)
+        nc.vector.reciprocal(out=pinv[:], in_=pn2c[:])
+        rp = const.tile([P, 1], F32)
+        nc.scalar.activation(out=rp[:], in_=pinv[:], func=ACT.Sqrt)
+
+        p_t = const.tile([P, PACK, P], BF16)
+        nc.vector.tensor_copy(out=p_t[:], in_=p_sb[:].rearrange("k (p t) -> k t p", t=PACK))
+        p_ps = rps.tile([P, PACK, P], BF16, tag="r_ps")
+        for t in range(PACK):
+            nc.tensor.transpose(p_ps[:, t, :], p_t[:, t, :], ident_b[:])
+        p_grp = const.tile([P, K, PACK], BF16, align_bytes=64)
+        nc.vector.tensor_copy(out=p_grp[:], in_=p_ps[:].rearrange("p t k -> p k t"))
+        p_codes = const.tile([P, K], U32, align_bytes=64)
+        p_scales = const.tile([P, K], U8, align_bytes=64)
+        nc.vector.quantize_mx(
+            out=p_codes[:].bitcast(FP8X4),
+            scales=p_scales[:],
+            in_=p_grp[:].rearrange("p k t -> p (k t)"),
+        )
+
+        state = {}
+
+        def norms(u):
+            raw = raws[u]
+            fn2 = small.tile([P, 2 * UNIT // GROUP], F32, name="fn2")
+            for g in range(UNIT // GROUP):
+                t_ps = tps.tile([P, PACK * P], F32, name="t_ps")
+                for t in range(PACK):
+                    words = raw[:, t, :].bitcast(F32)
+                    nc.tensor.transpose(
+                        t_ps[:, t * P:(t + 1) * P], words[:, g * P:(g + 1) * P], ident_f[:]
+                    )
+                halves = t_ps[:].bitcast(BF16).rearrange("m (c e) -> m c e", e=2)
+                for e in range(2):
+                    junk = junkp.tile([P, C], BF16, name="junk")
+                    nc.scalar.activation(
+                        out=junk[:], in_=halves[:, :, e], func=ACT.Square,
+                        accum_out=fn2[:, 2 * g + e:2 * g + e + 1],
+                    )
+            state[("fn2", u)] = fn2
+
+        def quantise(u):
+            raw = raws[u]
+            grp = grpp.tile([P, UNIT, PACK], BF16, name="grp", align_bytes=64)
+            nc.vector.tensor_copy(
+                out=grp[:].rearrange("p (c i) t -> p c t i", i=4),
+                in_=raw[:].rearrange("p t (c i) -> p c t i", i=4),
+            )
+            codes = codp.tile([P, UNIT], U32, name="codes", align_bytes=64)
+            scales = codp.tile([P, UNIT], U8, name="scales", align_bytes=64)
+            nc.vector.quantize_mx(
+                out=codes[:].bitcast(FP8X4),
+                scales=scales[:],
+                in_=grp[:].rearrange("p w t -> p (w t)"),
+            )
+            state[("codes", u)] = (codes, scales)
+
+        def inverse_norms(u):
+            fn2 = state[("fn2", u)]
+            n = 2 * UNIT // GROUP
+            fn2c = small.tile([P, n], F32, name="fn2c")
+            nc.vector.tensor_scalar(out=fn2c[:], in0=fn2[:], scalar1=TINY, scalar2=None, op0=ALU.max)
+            finv = small.tile([P, n], F32, name="finv")
+            nc.vector.reciprocal(out=finv[:], in_=fn2c[:])
+            rf = small.tile([P, n], F32, name="rf")
+            nc.scalar.activation(out=rf[:], in_=finv[:], func=ACT.Sqrt)
+            state[("rf", u)] = rf
+
+        def finish(u):
+            codes, scales = state[("codes", u)]
+            rf = state[("rf", u)]
+            b, off = divmod(u * UNIT, HW)
+            o_sb = op.tile([P, UNIT], F32, name="o_sb")
+            n_ch = UNIT // CHUNK
+            d_list = []
+            for ch in range(n_ch):
+                cols = slice(ch * CHUNK, (ch + 1) * CHUNK)
+                d_ps = dps.tile([P, CHUNK], F32, name="d_ps")
+                nc.tensor.matmul_mx(
+                    out=d_ps[:],
+                    lhsT=p_codes[:].bitcast(FP8X4),
+                    lhsT_scale=p_scales[:],
+                    rhs=codes[:, cols].bitcast(FP8X4),
+                    rhs_scale=scales[:, cols],
+                    start=True,
+                    stop=True,
+                )
+                d_list.append(d_ps)
+            for ch in range(n_ch):
+                r_ps = rps.tile([P, CHUNK], F32, name="r_ps", tag="r_ps")
+                for i in range(CHUNK // P):
+                    col = ch * (CHUNK // P) + i
+                    nc.tensor.transpose(
+                        r_ps[:, i * P:(i + 1) * P],
+                        rf[:, col:col + 1].to_broadcast([P, P]),
+                        ident_f[:],
+                    )
+                w_sb = wp.tile([P, CHUNK], F32, name="w_sb")
+                w_view = w_sb[:].rearrange("k (g m e) -> k g m e", m=P, e=2)
+                r_view = r_ps[:].rearrange("k (g e m) -> k g m e", m=P, e=2)
+                if (u * n_ch + ch) % 3 == 0:
+                    nc.scalar.activation(out=w_view, in_=r_view, func=ACT.Copy, scale=rp[:, 0:1])
+                else:
+                    nc.vector.tensor_scalar(
+                        out=w_view, in0=r_view, scalar1=rp[:, 0:1], scalar2=None, op0=ALU.mult
+                    )
+                nc.vector.scalar_tensor_tensor(
+                    out=o_sb[:, ch * CHUNK:(ch + 1) * CHUNK],
+                    in0=w_sb[:], scalar=1.0 / EPS, in1=d_list[ch][:],
+                    op0=ALU.min, op1=ALU.mult,
+                )
+            dst = out[b].rearrange("k h w -> k (h w)")
+            nc.sync.dma_start(out=dst[:, off:off + UNIT], in_=o_sb[:])
+
+        norms(0)
+        quantise(0)
+        for u in range(N_UNITS):
+            if u + 1 < N_UNITS:
+                norms(u + 1)
+                quantise(u + 1)
+            inverse_norms(u)
+            finish(u)

@@ -14,173 +14,278 @@ ALU = mybir.AluOpType
 P = 128
 PACK = 4
 B, C, HW, K = 4, 512, 4096, 128
-UNIT = 1024
 CHUNK = 512
 GROUP = 256
-N_UNITS = B * HW // UNIT
+WIDTHS = [[256, 256, 512, 1024, 1024, 1024], [1024] * 4, [1024] * 4, [1024, 1024, 1024, 512, 256, 256]]
 EPS = 1e-8
 TINY = 2.0 ** -116
+S_EVAC = [1, 0]
+GP_COLS = {}
+MANUAL = True
 
 FLOPS = 2 * B * HW * C * K
 
 
 def tile_globalprototype_kernel(tc, features, prototypes, out):
     nc = tc.nc
+    units = []
+    for b in range(B):
+        off = 0
+        for w in WIDTHS[b]:
+            units.append((b, off, w))
+            off += w
+        assert off == HW
+    n_units = len(units)
+    count = {}
+    for (b, off, w) in units:
+        count[w] = count.get(w, 0) + 1
+
     with ExitStack() as ctx:
         const = ctx.enter_context(tc.tile_pool(name="const", bufs=1))
-        rawp = ctx.enter_context(tc.tile_pool(name="rawp", bufs=N_UNITS))
+        rawp = ctx.enter_context(tc.tile_pool(name="rawp", bufs=1))
         grpp = ctx.enter_context(tc.tile_pool(name="grpp", bufs=2))
         codp = ctx.enter_context(tc.tile_pool(name="codp", bufs=3))
         small = ctx.enter_context(tc.tile_pool(name="small", bufs=4))
         junkp = ctx.enter_context(tc.tile_pool(name="junkp", bufs=2))
         wp = ctx.enter_context(tc.tile_pool(name="wp", bufs=4))
-        op = ctx.enter_context(tc.tile_pool(name="op", bufs=3))
+        op = ctx.enter_context(tc.tile_pool(name="op", bufs=6))
         tps = ctx.enter_context(tc.psum_pool(name="tps", bufs=4))
         rps = ctx.enter_context(tc.psum_pool(name="rps", bufs=2))
         dps = ctx.enter_context(tc.psum_pool(name="dps", bufs=2))
+        if MANUAL:
+            ctx.enter_context(tc.manual_schedule())
 
-        p_sb = const.tile([P, C], BF16)
-        nc.scalar.dma_start(out=p_sb[:], in_=prototypes)
         raws = []
-        for u in range(N_UNITS):
-            b, off = divmod(u * UNIT, HW)
-            raw = rawp.tile([P, PACK, UNIT], BF16, name="raw")
+
+        def load(u):
+            b, off, w = units[u]
+            raw = rawp.tile([P, PACK, w], BF16, name="raw%d" % w, tag="raw%d" % w, bufs=count[w])
             src = features[b].rearrange("(p j) h w -> p j (h w)", j=PACK)
-            nc.sync.dma_start(out=raw[:], in_=src[:, :, off:off + UNIT])
+            nc.sync.dma_start(out=raw[:], in_=src[:, :, off:off + w])
             raws.append(raw)
 
+        p_sb = const.tile([P, C], BF16)
+        LOADS_AHEAD = 7
+        load(0)
+        nc.sync.dma_start(out=p_sb[:], in_=prototypes)
+        for u in range(1, LOADS_AHEAD):
+            load(u)
+
+        tiny = const.tile([P, 1], F32)
+        nc.vector.memset(tiny[:], TINY)
         warm = const.tile([P, 1], F32)
-        nc.vector.memset(warm[:], 1.0)
-        nc.scalar.activation(out=warm[:], in_=warm[:], func=ACT.Sqrt)
+        nc.scalar.activation(out=warm[:], in_=tiny[:], func=ACT.Sqrt, bias=tiny[:, 0:1])
         ident_f = const.tile([P, P], F32)
         make_identity(nc, ident_f[:])
         ident_b = const.tile([P, P], BF16)
         make_identity(nc, ident_b[:])
 
-        pjunk = junkp.tile([P, C], BF16, name="junk")
-        pn2 = const.tile([P, 1], F32)
-        nc.scalar.activation(out=pjunk[:], in_=p_sb[:], func=ACT.Square, accum_out=pn2[:])
-        pn2c = const.tile([P, 1], F32)
-        nc.vector.tensor_scalar(out=pn2c[:], in0=pn2[:], scalar1=TINY, scalar2=None, op0=ALU.max)
-        pinv = const.tile([P, 1], F32)
-        nc.vector.reciprocal(out=pinv[:], in_=pn2c[:])
-        rp = const.tile([P, 1], F32)
-        nc.scalar.activation(out=rp[:], in_=pinv[:], func=ACT.Sqrt)
-
-        p_t = const.tile([P, PACK, P], BF16)
-        nc.vector.tensor_copy(out=p_t[:], in_=p_sb[:].rearrange("k (p t) -> k t p", t=PACK))
-        p_ps = rps.tile([P, PACK, P], BF16, tag="r_ps")
-        for t in range(PACK):
-            nc.tensor.transpose(p_ps[:, t, :], p_t[:, t, :], ident_b[:])
-        p_grp = const.tile([P, K, PACK], BF16, align_bytes=64)
-        nc.vector.tensor_copy(out=p_grp[:], in_=p_ps[:].rearrange("p t k -> p k t"))
-        p_codes = const.tile([P, K], U32, align_bytes=64)
-        p_scales = const.tile([P, K], U8, align_bytes=64)
-        nc.vector.quantize_mx(
-            out=p_codes[:].bitcast(FP8X4),
-            scales=p_scales[:],
-            in_=p_grp[:].rearrange("p k t -> p (k t)"),
-        )
-
         state = {}
 
-        def norms(u):
+        def prototypes_turn():
+            p_t = const.tile([P, PACK, P], BF16)
+            nc.vector.tensor_copy(out=p_t[:], in_=p_sb[:].rearrange("k (p t) -> k t p", t=PACK))
+            p_ps = rps.tile([P, PACK, P], BF16, tag="r_ps")
+            for t in range(PACK):
+                nc.tensor.transpose(p_ps[:, t, :], p_t[:, t, :], ident_b[:])
+            state["p_ps"] = p_ps
+
+        def prototypes_finish():
+            pjunk = junkp.tile([P, C], BF16, name="junk")
+            pn2 = const.tile([P, 1], F32)
+            nc.scalar.activation(out=pjunk[:], in_=p_sb[:], func=ACT.Square, accum_out=pn2[:])
+            pn = const.tile([P, 1], F32)
+            nc.scalar.activation(out=pn[:], in_=pn2[:], func=ACT.Sqrt, bias=tiny[:, 0:1])
+            p_grp = const.tile([P, K, PACK], BF16, align_bytes=64)
+            nc.vector.tensor_copy(out=p_grp[:], in_=state["p_ps"][:].rearrange("p t k -> p k t"))
+            rp = const.tile([P, 1], F32)
+            nc.vector.reciprocal(out=rp[:], in_=pn[:])
+            p_codes = const.tile([P, K], U32, align_bytes=64)
+            p_scales = const.tile([P, K], U8, align_bytes=64)
+            nc.vector.quantize_mx(
+                out=p_codes[:].bitcast(FP8X4),
+                scales=p_scales[:],
+                in_=p_grp[:].rearrange("p k t -> p (k t)"),
+            )
+            state["p"] = (p_codes, p_scales, rp)
+
+        def transposes(u, g):
             raw = raws[u]
-            fn2 = small.tile([P, 2 * UNIT // GROUP], F32, name="fn2")
-            for g in range(UNIT // GROUP):
-                t_ps = tps.tile([P, PACK * P], F32, name="t_ps")
-                for t in range(PACK):
-                    words = raw[:, t, :].bitcast(F32)
-                    nc.tensor.transpose(
-                        t_ps[:, t * P:(t + 1) * P], words[:, g * P:(g + 1) * P], ident_f[:]
-                    )
-                halves = t_ps[:].bitcast(BF16).rearrange("m (c e) -> m c e", e=2)
-                for e in range(2):
-                    junk = junkp.tile([P, C], BF16, name="junk")
-                    nc.scalar.activation(
-                        out=junk[:], in_=halves[:, :, e], func=ACT.Square,
-                        accum_out=fn2[:, 2 * g + e:2 * g + e + 1],
-                    )
-            state[("fn2", u)] = fn2
+            t_ps = tps.tile([P, PACK * P], F32, name="t_ps")
+            for t in range(PACK):
+                words = raw[:, t, :].bitcast(F32)
+                nc.tensor.transpose(t_ps[:, t * P:(t + 1) * P], words[:, g * P:(g + 1) * P], ident_f[:])
+            state[("t", u, g)] = t_ps
+
+        def squares(u, g):
+            if g == 0:
+                fn2_new = small.tile([P, 8], F32, name="fn2")
+                state[("fn2", u)] = fn2_new
+            fn2 = state[("fn2", u)]
+            t_ps = state[("t", u, g)]
+            halves = t_ps[:].bitcast(BF16).rearrange("m (c e) -> m c e", e=2)
+            for e in range(2):
+                junk = junkp.tile([P, C], BF16, name="junk")
+                nc.scalar.activation(
+                    out=junk[:], in_=halves[:, :, e], func=ACT.Square,
+                    accum_out=fn2[:, 2 * g + e:2 * g + e + 1],
+                )
+
+        def root(u):
+            n = 2 * units[u][2] // GROUP
+            fn = small.tile([P, 8], F32, name="fn")
+            nc.scalar.activation(out=fn[:, :n], in_=state[("fn2", u)][:, :n], func=ACT.Sqrt, bias=tiny[:, 0:1])
+            state[("fn", u)] = fn
+
+        def invert(u):
+            n = 2 * units[u][2] // GROUP
+            rf = small.tile([P, 8], F32, name="rf")
+            nc.vector.reciprocal(out=rf[:, :n], in_=state[("fn", u)][:, :n])
+            state[("rf", u)] = rf
+
+        def regroup(u):
+            w = units[u][2]
+            raw = raws[u]
+            grp = grpp.tile([P, w, PACK], BF16, name="grp", tag="grp", align_bytes=64)
+            gp = GP_COLS.get(w, 0)
+            v = w - gp
+            nc.vector.tensor_copy(
+                out=grp[:, :v, :].rearrange("p (c i) t -> p c t i", i=4),
+                in_=raw[:, :, :v].rearrange("p t (c i) -> p c t i", i=4),
+            )
+            if gp:
+                nc.gpsimd.tensor_scalar(
+                    out=grp[:, v:, :], in0=raw[:, :, v:].rearrange("p t c -> p c t"),
+                    scalar1=1.0, scalar2=0.0, op0=ALU.mult, op1=ALU.add,
+                )
+            state[("grp", u)] = grp
 
         def quantise(u):
-            raw = raws[u]
-            grp = grpp.tile([P, UNIT, PACK], BF16, name="grp", align_bytes=64)
-            nc.vector.tensor_copy(
-                out=grp[:].rearrange("p (c i) t -> p c t i", i=4),
-                in_=raw[:].rearrange("p t (c i) -> p c t i", i=4),
-            )
-            codes = codp.tile([P, UNIT], U32, name="codes", align_bytes=64)
-            scales = codp.tile([P, UNIT], U8, name="scales", align_bytes=64)
+            w = units[u][2]
+            grp = state[("grp", u)]
+            codes = codp.tile([P, w], U32, name="codes", tag="codes", align_bytes=64)
+            scales = codp.tile([P, w], U8, name="scales", tag="scales", align_bytes=64)
             nc.vector.quantize_mx(
-                out=codes[:].bitcast(FP8X4),
-                scales=scales[:],
-                in_=grp[:].rearrange("p w t -> p (w t)"),
+                out=codes[:].bitcast(FP8X4), scales=scales[:], in_=grp[:].rearrange("p w t -> p (w t)"),
             )
             state[("codes", u)] = (codes, scales)
 
-        def inverse_norms(u):
-            fn2 = state[("fn2", u)]
-            n = 2 * UNIT // GROUP
-            fn2c = small.tile([P, n], F32, name="fn2c")
-            nc.vector.tensor_scalar(out=fn2c[:], in0=fn2[:], scalar1=TINY, scalar2=None, op0=ALU.max)
-            finv = small.tile([P, n], F32, name="finv")
-            nc.vector.reciprocal(out=finv[:], in_=fn2c[:])
-            rf = small.tile([P, n], F32, name="rf")
-            nc.scalar.activation(out=rf[:], in_=finv[:], func=ACT.Sqrt)
-            state[("rf", u)] = rf
+        def chunks(u):
+            w = units[u][2]
+            cw = min(w, CHUNK)
+            return [(c * cw, cw) for c in range(w // cw)]
 
-        def finish(u):
+        def dots(u):
             codes, scales = state[("codes", u)]
-            rf = state[("rf", u)]
-            b, off = divmod(u * UNIT, HW)
-            o_sb = op.tile([P, UNIT], F32, name="o_sb")
-            n_ch = UNIT // CHUNK
-            d_list = []
-            for ch in range(n_ch):
-                cols = slice(ch * CHUNK, (ch + 1) * CHUNK)
-                d_ps = dps.tile([P, CHUNK], F32, name="d_ps")
+            p_codes, p_scales, rp = state["p"]
+            for (c0, cw) in chunks(u):
+                d_ps = dps.tile([P, cw], F32, name="d_ps", tag="d_ps")
                 nc.tensor.matmul_mx(
                     out=d_ps[:],
-                    lhsT=p_codes[:].bitcast(FP8X4),
-                    lhsT_scale=p_scales[:],
-                    rhs=codes[:, cols].bitcast(FP8X4),
-                    rhs_scale=scales[:, cols],
-                    start=True,
-                    stop=True,
+                    lhsT=p_codes[:].bitcast(FP8X4), lhsT_scale=p_scales[:],
+                    rhs=codes[:, c0:c0 + cw].bitcast(FP8X4), rhs_scale=scales[:, c0:c0 + cw],
+                    start=True, stop=True,
                 )
-                d_list.append(d_ps)
-            for ch in range(n_ch):
-                r_ps = rps.tile([P, CHUNK], F32, name="r_ps", tag="r_ps")
-                for i in range(CHUNK // P):
-                    col = ch * (CHUNK // P) + i
-                    nc.tensor.transpose(
-                        r_ps[:, i * P:(i + 1) * P],
-                        rf[:, col:col + 1].to_broadcast([P, P]),
-                        ident_f[:],
-                    )
-                w_sb = wp.tile([P, CHUNK], F32, name="w_sb")
-                w_view = w_sb[:].rearrange("k (g m e) -> k g m e", m=P, e=2)
-                r_view = r_ps[:].rearrange("k (g e m) -> k g m e", m=P, e=2)
-                if (u * n_ch + ch) % 3 == 0:
-                    nc.scalar.activation(out=w_view, in_=r_view, func=ACT.Copy, scale=rp[:, 0:1])
-                else:
-                    nc.vector.tensor_scalar(
-                        out=w_view, in0=r_view, scalar1=rp[:, 0:1], scalar2=None, op0=ALU.mult
-                    )
-                nc.vector.scalar_tensor_tensor(
-                    out=o_sb[:, ch * CHUNK:(ch + 1) * CHUNK],
-                    in0=w_sb[:], scalar=1.0 / EPS, in1=d_list[ch][:],
-                    op0=ALU.min, op1=ALU.mult,
-                )
-            dst = out[b].rearrange("k h w -> k (h w)")
-            nc.sync.dma_start(out=dst[:, off:off + UNIT], in_=o_sb[:])
+                state[("d", u, c0)] = d_ps
 
-        norms(0)
-        quantise(0)
-        for u in range(N_UNITS):
-            if u + 1 < N_UNITS:
-                norms(u + 1)
-                quantise(u + 1)
-            inverse_norms(u)
-            finish(u)
+        def spread(u, c0, cw):
+            rf = state[("rf", u)]
+            r_ps = rps.tile([P, cw], F32, name="r_ps", tag="r_ps")
+            for i in range(cw // P):
+                col = c0 // P + i
+                nc.tensor.transpose(r_ps[:, i * P:(i + 1) * P], rf[:, col:col + 1].to_broadcast([P, P]), ident_f[:])
+            state[("r", u, c0)] = r_ps
+
+        def evacuate(u, c0, cw, on_scalar):
+            rp = state["p"][2]
+            r_ps = state[("r", u, c0)]
+            w_sb = wp.tile([P, cw], F32, name="w_sb", tag="w_sb")
+            w_view = w_sb[:].rearrange("k (g m e) -> k g m e", m=P, e=2)
+            r_view = r_ps[:].rearrange("k (g e m) -> k g m e", m=P, e=2)
+            if on_scalar:
+                nc.scalar.activation(out=w_view, in_=r_view, func=ACT.Copy, scale=rp[:, 0:1])
+            else:
+                nc.vector.tensor_scalar(out=w_view, in0=r_view, scalar1=rp[:, 0:1], scalar2=None, op0=ALU.mult)
+            state[("w", u, c0)] = w_sb
+
+        def scale(u, c0, cw):
+            if c0 == 0:
+                o_new = op.tile([P, units[u][2]], F32, name="o_sb", tag="o_sb")
+                state[("o", u)] = o_new
+            o_sb = state[("o", u)]
+            nc.vector.scalar_tensor_tensor(
+                out=o_sb[:, c0:c0 + cw], in0=state[("w", u, c0)][:], scalar=1.0 / EPS,
+                in1=state[("d", u, c0)][:], op0=ALU.min, op1=ALU.mult,
+            )
+
+        def store(u, c0, cw):
+            b, off, w = units[u]
+            dst = out[b].rearrange("k h w -> k (h w)")
+            nc.sync.dma_start(out=dst[:, off + c0:off + c0 + cw], in_=state[("o", u)][:, c0:c0 + cw])
+
+        n_evac = [0]
+
+        def on_scalar():
+            n_evac[0] += 1
+            return S_EVAC[n_evac[0] % len(S_EVAC)] == 1
+
+        slots = []
+        first = {}
+        last = {}
+        for u in range(n_units):
+            for g in range(units[u][2] // GROUP):
+                if g == 0:
+                    first[u] = len(slots)
+                last[u] = len(slots)
+                slots.append((u, g))
+        n_slots = len(slots)
+        AHEAD = 3
+        TAIL = 12
+        events = [[] for s in range(n_slots + TAIL)]
+        for u in range(n_units):
+            f, l = first[u], last[u]
+            events[f + 0].append((5.0, "regroup", u, 0, 0))
+            events[max(f + 0, l + 0)].append((6.0, "quantise", u, 0, 0))
+            events[l + 1].append((0.0, "invert", u, 0, 0))
+            events[l + 1].append((1.0, "dots", u, 0, 0))
+            for i, (c0, cw) in enumerate(chunks(u)):
+                events[l + 1].append((2.0, "spread", u, c0, cw))
+                if i == 0:
+                    events[l + 3].append((3.0, "evacuate", u, c0, cw))
+                    events[l + 3].append((4.0, "scale", u, c0, cw))
+                else:
+                    events[l + 3].append((3.0, "evacuate", u, c0, cw))
+                    events[l + 4].append((7.0, "scale", u, c0, cw))
+
+        for s in range(min(AHEAD, n_slots)):
+            transposes(slots[s][0], slots[s][1])
+            if s == 0:
+                prototypes_turn()
+        for s in range(n_slots + TAIL):
+            if s + AHEAD < n_slots:
+                transposes(slots[s + AHEAD][0], slots[s + AHEAD][1])
+            if s < n_slots:
+                u, g = slots[s]
+                if g == 0 and u + LOADS_AHEAD < n_units:
+                    load(u + LOADS_AHEAD)
+                squares(u, g)
+                if s == last[u]:
+                    root(u)
+            for (rank, kind, u, c0, cw) in sorted(events[s]):
+                if kind == "regroup":
+                    regroup(u)
+                elif kind == "quantise":
+                    quantise(u)
+                elif kind == "invert":
+                    invert(u)
+                elif kind == "dots":
+                    dots(u)
+                elif kind == "spread":
+                    spread(u, c0, cw)
+                elif kind == "evacuate":
+                    evacuate(u, c0, cw, (c0 > 0 and u % 5 != 4) or u >= n_units - 3)
+                else:
+                    scale(u, c0, cw)
+                    store(u, c0, cw)
+            if s == 0:
+                prototypes_finish()

@@ -20,7 +20,7 @@ WIDTHS = [[256, 256, 512, 1024, 1024, 1024], [1024] * 4, [1024] * 4, [1024, 1024
 EPS = 1e-8
 TINY = 2.0 ** -116
 S_EVAC = [1, 0]
-GP_COLS = {}
+GP_COLS = {1024: 384}
 MANUAL = True
 
 FLOPS = 2 * B * HW * C * K
@@ -43,7 +43,7 @@ def tile_globalprototype_kernel(tc, features, prototypes, out):
     with ExitStack() as ctx:
         const = ctx.enter_context(tc.tile_pool(name="const", bufs=1))
         rawp = ctx.enter_context(tc.tile_pool(name="rawp", bufs=1))
-        grpp = ctx.enter_context(tc.tile_pool(name="grpp", bufs=2))
+        grpp = ctx.enter_context(tc.tile_pool(name="grpp", bufs=3))
         codp = ctx.enter_context(tc.tile_pool(name="codp", bufs=3))
         small = ctx.enter_context(tc.tile_pool(name="small", bufs=4))
         junkp = ctx.enter_context(tc.tile_pool(name="junkp", bufs=2))
@@ -244,18 +244,16 @@ def tile_globalprototype_kernel(tc, features, prototypes, out):
         events = [[] for s in range(n_slots + TAIL)]
         for u in range(n_units):
             f, l = first[u], last[u]
-            events[f + 0].append((5.0, "regroup", u, 0, 0))
-            events[max(f + 0, l + 0)].append((6.0, "quantise", u, 0, 0))
+            events[max(0, f - 1)].append((5.0, "regroup", u, 0, 0))
+            events[l].append((6.0, "quantise", u, 0, 0))
             events[l + 1].append((0.0, "invert", u, 0, 0))
-            events[l + 1].append((1.0, "dots", u, 0, 0))
+            events[l + 1].append((0.5, "dots", u, 0, 0))
             for i, (c0, cw) in enumerate(chunks(u)):
-                events[l + 1].append((2.0, "spread", u, c0, cw))
+                events[l + 1].append((0.6, "spread", u, c0, cw))
                 if i == 0:
-                    events[l + 3].append((3.0, "evacuate", u, c0, cw))
-                    events[l + 3].append((4.0, "scale", u, c0, cw))
+                    events[l + 2].append((3.0, "finish", u, c0, cw))
                 else:
-                    events[l + 3].append((3.0, "evacuate", u, c0, cw))
-                    events[l + 4].append((7.0, "scale", u, c0, cw))
+                    events[l + 5].append((1.0, "finish", u, c0, cw))
 
         for s in range(min(AHEAD, n_slots)):
             transposes(slots[s][0], slots[s][1])
@@ -282,9 +280,8 @@ def tile_globalprototype_kernel(tc, features, prototypes, out):
                     dots(u)
                 elif kind == "spread":
                     spread(u, c0, cw)
-                elif kind == "evacuate":
-                    evacuate(u, c0, cw, (c0 > 0 and u % 5 != 4) or u >= n_units - 3)
                 else:
+                    evacuate(u, c0, cw, u >= n_units - 3)
                     scale(u, c0, cw)
                     store(u, c0, cw)
             if s == 0:

@@ -244,16 +244,13 @@ def tile_globalprototype_kernel(tc, features, prototypes, out):
         events = [[] for s in range(n_slots + TAIL)]
         for u in range(n_units):
             f, l = first[u], last[u]
-            events[max(0, f - 1)].append((5.0, "regroup", u, 0, 0))
-            events[l].append((6.0, "quantise", u, 0, 0))
+            events[last[u - 2] + 1 if u >= 2 else 0].append((5.0, "regroup", u, 0, 0))
+            events[f].append((6.0, "quantise", u, 0, 0))
             events[l + 1].append((0.0, "invert", u, 0, 0))
             events[l + 1].append((0.5, "dots", u, 0, 0))
             for i, (c0, cw) in enumerate(chunks(u)):
                 events[l + 1].append((0.6, "spread", u, c0, cw))
-                if i == 0:
-                    events[l + 2].append((3.0, "finish", u, c0, cw))
-                else:
-                    events[l + 5].append((1.0, "finish", u, c0, cw))
+                events[l + 2].append((7.0 + i, "finish", u, c0, cw))
 
         for s in range(min(AHEAD, n_slots)):
             transposes(slots[s][0], slots[s][1])

@@ -20,7 +20,7 @@ WIDTHS = [[256, 256, 512, 1024, 1024, 1024], [1024] * 4, [1024] * 4, [1024, 1024
 EPS = 1e-8
 TINY = 2.0 ** -116
 S_EVAC = [1, 0]
-GP_COLS = {1024: 384}
+GP_COLS = {1024: 448}
 MANUAL = True
 
 FLOPS = 2 * B * HW * C * K
@@ -247,10 +247,11 @@ def tile_globalprototype_kernel(tc, features, prototypes, out):
             events[last[u - 2] + 1 if u >= 2 else 0].append((5.0, "regroup", u, 0, 0))
             events[f].append((6.0, "quantise", u, 0, 0))
             events[l + 1].append((0.0, "invert", u, 0, 0))
-            events[l + 1].append((0.5, "dots", u, 0, 0))
+            events[l + 1].append((0.7, "dots", u, 0, 0))
             for i, (c0, cw) in enumerate(chunks(u)):
                 events[l + 1].append((0.6, "spread", u, c0, cw))
-                events[l + 2].append((7.0 + i, "finish", u, c0, cw))
+                events[l + 2].append((7.0 + i, "evacuate", u, c0, cw))
+                events[l + 2].append((8.0 + i, "scale", u, c0, cw))
 
         for s in range(min(AHEAD, n_slots)):
             transposes(slots[s][0], slots[s][1])
@@ -277,8 +278,9 @@ def tile_globalprototype_kernel(tc, features, prototypes, out):
                     dots(u)
                 elif kind == "spread":
                     spread(u, c0, cw)
-                else:
+                elif kind == "evacuate":
                     evacuate(u, c0, cw, u >= n_units - 3)
+                else:
                     scale(u, c0, cw)
                     store(u, c0, cw)
             if s == 0:

@@ -20,7 +20,20 @@ WIDTHS = [[256, 256, 512, 1024, 1024, 1024], [1024] * 4, [1024] * 4, [1024, 1024
 EPS = 1e-8
 TINY = 2.0 ** -116
 S_EVAC = [1, 0]
-GP_COLS = {1024: 448}
+GP_COLS = {1024: 304}
+GRAM_UNITS = []
+SC_FROM = 3
+EV = 2
+SEV = 4
+GP_FROM = 4
+CB = 3
+GB = 3
+DG = 2
+GA = 4
+RA = 2
+QA = 0
+SPR = 2
+SC_CH = [(u, 512) for u in range(5, 17, 2)]
 MANUAL = True
 
 FLOPS = 2 * B * HW * C * K
@@ -43,15 +56,14 @@ def tile_globalprototype_kernel(tc, features, prototypes, out):
     with ExitStack() as ctx:
         const = ctx.enter_context(tc.tile_pool(name="const", bufs=1))
         rawp = ctx.enter_context(tc.tile_pool(name="rawp", bufs=1))
-        grpp = ctx.enter_context(tc.tile_pool(name="grpp", bufs=3))
-        codp = ctx.enter_context(tc.tile_pool(name="codp", bufs=3))
+        grpp = ctx.enter_context(tc.tile_pool(name="grpp", bufs=GB))
+        codp = ctx.enter_context(tc.tile_pool(name="codp", bufs=CB))
         small = ctx.enter_context(tc.tile_pool(name="small", bufs=4))
         junkp = ctx.enter_context(tc.tile_pool(name="junkp", bufs=2))
         wp = ctx.enter_context(tc.tile_pool(name="wp", bufs=4))
         op = ctx.enter_context(tc.tile_pool(name="op", bufs=6))
         tps = ctx.enter_context(tc.psum_pool(name="tps", bufs=4))
-        rps = ctx.enter_context(tc.psum_pool(name="rps", bufs=2))
-        dps = ctx.enter_context(tc.psum_pool(name="dps", bufs=2))
+        rps = ctx.enter_context(tc.psum_pool(name="rps", bufs=4))
         if MANUAL:
             ctx.enter_context(tc.manual_schedule())
 
@@ -85,7 +97,7 @@ def tile_globalprototype_kernel(tc, features, prototypes, out):
         def prototypes_turn():
             p_t = const.tile([P, PACK, P], BF16)
             nc.vector.tensor_copy(out=p_t[:], in_=p_sb[:].rearrange("k (p t) -> k t p", t=PACK))
-            p_ps = rps.tile([P, PACK, P], BF16, tag="r_ps")
+            p_ps = rps.tile([P, PACK, P], BF16, name="x_ps", tag="x_ps")
             for t in range(PACK):
                 nc.tensor.transpose(p_ps[:, t, :], p_t[:, t, :], ident_b[:])
             state["p_ps"] = p_ps
@@ -117,11 +129,36 @@ def tile_globalprototype_kernel(tc, features, prototypes, out):
                 nc.tensor.transpose(t_ps[:, t * P:(t + 1) * P], words[:, g * P:(g + 1) * P], ident_f[:])
             state[("t", u, g)] = t_ps
 
-        def squares(u, g):
-            if g == 0:
+        def gram(u, g):
+            raw = raws[u]
+            g_ps = rps.tile([P, 2 * P], F32, name="x_ps", tag="x_ps")
+            for e in range(2):
+                cols = slice(g * GROUP + e, (g + 1) * GROUP, 2)
+                for t in range(PACK):
+                    nc.tensor.matmul(
+                        g_ps[:, e * P:(e + 1) * P], lhsT=raw[:, t, cols], rhs=raw[:, t, cols],
+                        start=(t == 0), stop=(t == PACK - 1),
+                    )
+            state[("t", u, g)] = g_ps
+
+        def norms(u):
+            if ("fn2", u) not in state:
                 fn2_new = small.tile([P, 8], F32, name="fn2")
                 state[("fn2", u)] = fn2_new
-            fn2 = state[("fn2", u)]
+            return state[("fn2", u)]
+
+        def diagonals(u, g):
+            fn2 = norms(u)
+            g_ps = state[("t", u, g)]
+            for e in range(2):
+                junk = junkp.tile([P, P], F32, name="gjunk")
+                nc.vector.scalar_tensor_tensor(
+                    out=junk[:], in0=g_ps[:, e * P:(e + 1) * P], scalar=1.0, in1=ident_f[:], op0=ALU.mult, op1=ALU.mult,
+                    accum_out=fn2[:, 2 * g + e:2 * g + e + 1],
+                )
+
+        def squares(u, g, pending):
+            fn2 = norms(u)
             t_ps = state[("t", u, g)]
             halves = t_ps[:].bitcast(BF16).rearrange("m (c e) -> m c e", e=2)
             for e in range(2):
@@ -130,6 +167,8 @@ def tile_globalprototype_kernel(tc, features, prototypes, out):
                     out=junk[:], in_=halves[:, :, e], func=ACT.Square,
                     accum_out=fn2[:, 2 * g + e:2 * g + e + 1],
                 )
+                while pending:
+                    root(pending.pop(0))
 
         def root(u):
             n = 2 * units[u][2] // GROUP
@@ -147,7 +186,7 @@ def tile_globalprototype_kernel(tc, features, prototypes, out):
             w = units[u][2]
             raw = raws[u]
             grp = grpp.tile([P, w, PACK], BF16, name="grp", tag="grp", align_bytes=64)
-            gp = GP_COLS.get(w, 0)
+            gp = GP_COLS.get(w, 0) if u >= GP_FROM else 0
             v = w - gp
             nc.vector.tensor_copy(
                 out=grp[:, :v, :].rearrange("p (c i) t -> p c t i", i=4),
@@ -179,7 +218,7 @@ def tile_globalprototype_kernel(tc, features, prototypes, out):
             codes, scales = state[("codes", u)]
             p_codes, p_scales, rp = state["p"]
             for (c0, cw) in chunks(u):
-                d_ps = dps.tile([P, cw], F32, name="d_ps", tag="d_ps")
+                d_ps = rps.tile([P, cw], F32, name="x_ps", tag="x_ps")
                 nc.tensor.matmul_mx(
                     out=d_ps[:],
                     lhsT=p_codes[:].bitcast(FP8X4), lhsT_scale=p_scales[:],
@@ -190,7 +229,7 @@ def tile_globalprototype_kernel(tc, features, prototypes, out):
 
         def spread(u, c0, cw):
             rf = state[("rf", u)]
-            r_ps = rps.tile([P, cw], F32, name="r_ps", tag="r_ps")
+            r_ps = rps.tile([P, cw], F32, name="x_ps", tag="x_ps")
             for i in range(cw // P):
                 col = c0 // P + i
                 nc.tensor.transpose(r_ps[:, i * P:(i + 1) * P], rf[:, col:col + 1].to_broadcast([P, P]), ident_f[:])
@@ -209,7 +248,7 @@ def tile_globalprototype_kernel(tc, features, prototypes, out):
             state[("w", u, c0)] = w_sb
 
         def scale(u, c0, cw):
-            if c0 == 0:
+            if ("o", u) not in state:
                 o_new = op.tile([P, units[u][2]], F32, name="o_sb", tag="o_sb")
                 state[("o", u)] = o_new
             o_sb = state[("o", u)]
@@ -239,37 +278,59 @@ def tile_globalprototype_kernel(tc, features, prototypes, out):
                 last[u] = len(slots)
                 slots.append((u, g))
         n_slots = len(slots)
+        gram_units = GRAM_UNITS
+        gram_slots = [(u, units[u][2] // GROUP - 1) for u in gram_units]
+
+        def turn(u, g):
+            if (u, g) not in gram_slots:
+                transposes(u, g)
+
         AHEAD = 3
-        TAIL = 12
+        TAIL = 16
         events = [[] for s in range(n_slots + TAIL)]
         for u in range(n_units):
             f, l = first[u], last[u]
-            events[last[u - 2] + 1 if u >= 2 else 0].append((5.0, "regroup", u, 0, 0))
-            events[f].append((6.0, "quantise", u, 0, 0))
+            if u in gram_units:
+                events[f - GA].append((9.6, "gram", u, 0, 0))
+                events[f - GA + DG].append((9.5, "diagonals", u, 0, 0))
+            events[last[u - RA] + 1 if u >= RA else 0].append((5.0, "regroup", u, 0, 0))
+            events[first[u - QA] if u >= QA else 0].append((6.0, "quantise", u, 0, 0))
             events[l + 1].append((0.0, "invert", u, 0, 0))
-            events[l + 1].append((0.7, "dots", u, 0, 0))
+            events[l + SPR].append((0.7, "dots", u, 0, 0))
             for i, (c0, cw) in enumerate(chunks(u)):
-                events[l + 1].append((0.6, "spread", u, c0, cw))
-                events[l + 2].append((7.0 + i, "evacuate", u, c0, cw))
-                events[l + 2].append((8.0 + i, "scale", u, c0, cw))
+                events[l + SPR].append((0.6, "spread", u, c0, cw))
+                late = (u, 512) in SC_CH
+                ev = SEV if (u, c0) in SC_CH else EV
+                sv = SEV if late else EV
+                events[l + ev].append((7.0 + i, "evacuate", u, c0, cw))
+                events[l + sv].append((8.0 + (1 - i if late else i), "scale", u, c0, cw))
 
+        pending = []
         for s in range(min(AHEAD, n_slots)):
-            transposes(slots[s][0], slots[s][1])
+            turn(slots[s][0], slots[s][1])
             if s == 0:
                 prototypes_turn()
         for s in range(n_slots + TAIL):
             if s + AHEAD < n_slots:
-                transposes(slots[s + AHEAD][0], slots[s + AHEAD][1])
+                turn(slots[s + AHEAD][0], slots[s + AHEAD][1])
             if s < n_slots:
                 u, g = slots[s]
                 if g == 0 and u + LOADS_AHEAD < n_units:
                     load(u + LOADS_AHEAD)
-                squares(u, g)
+                if (u, g) not in gram_slots:
+                    squares(u, g, pending)
                 if s == last[u]:
-                    root(u)
+                    pending.append(u)
+            else:
+                while pending:
+                    root(pending.pop(0))
             for (rank, kind, u, c0, cw) in sorted(events[s]):
                 if kind == "regroup":
                     regroup(u)
+                elif kind == "gram":
+                    gram(u, units[u][2] // GROUP - 1)
+                elif kind == "diagonals":
+                    diagonals(u, units[u][2] // GROUP - 1)
                 elif kind == "quantise":
                     quantise(u)
                 elif kind == "invert":
@@ -279,7 +340,7 @@ def tile_globalprototype_kernel(tc, features, prototypes, out):
                 elif kind == "spread":
                     spread(u, c0, cw)
                 elif kind == "evacuate":
-                    evacuate(u, c0, cw, u >= n_units - 3)
+                    evacuate(u, c0, cw, ((u, c0) in SC_CH) or u >= n_units - SC_FROM)
                 else:
                     scale(u, c0, cw)
                     store(u, c0, cw)

@@ -20,20 +20,20 @@ WIDTHS = [[256, 256, 512, 1024, 1024, 1024], [1024] * 4, [1024] * 4, [1024, 1024
 EPS = 1e-8
 TINY = 2.0 ** -116
 S_EVAC = [1, 0]
-GP_COLS = {1024: 304}
-GRAM_UNITS = []
+GP_COLS = {1024: 448}
+GRAM_UNITS = [4, 6, 8, 10, 12, 14]
 SC_FROM = 3
-EV = 2
+EV = 3
 SEV = 4
 GP_FROM = 4
 CB = 3
 GB = 3
-DG = 2
-GA = 4
+DG = 1
+GA = 2
 RA = 2
 QA = 0
 SPR = 2
-SC_CH = [(u, 512) for u in range(5, 17, 2)]
+SC_CH = [(u, 512) for u in range(4, 17, 2)]
 MANUAL = True
 
 FLOPS = 2 * B * HW * C * K

@@ -20,12 +20,12 @@ WIDTHS = [[256, 256, 512, 1024, 1024, 1024], [1024] * 4, [1024] * 4, [1024, 1024
 EPS = 1e-8
 TINY = 2.0 ** -116
 S_EVAC = [1, 0]
-GP_COLS = {1024: 448}
-GRAM_UNITS = [4, 6, 8, 10, 12, 14]
+GP_COLS = {1024: 416}
+GRAM_UNITS = [6, 8, 10, 12, 14, 16]
 SC_FROM = 3
 EV = 3
 SEV = 4
-GP_FROM = 4
+GP_FROM = 0
 CB = 3
 GB = 3
 DG = 1
@@ -133,7 +133,7 @@ def tile_globalprototype_kernel(tc, features, prototypes, out):
             raw = raws[u]
             g_ps = rps.tile([P, 2 * P], F32, name="x_ps", tag="x_ps")
             for e in range(2):
-                cols = slice(g * GROUP + e, (g + 1) * GROUP, 2)
+                cols = slice(g * GROUP + e * P, g * GROUP + (e + 1) * P)
                 for t in range(PACK):
                     nc.tensor.matmul(
                         g_ps[:, e * P:(e + 1) * P], lhsT=raw[:, t, cols], rhs=raw[:, t, cols],
@@ -157,7 +157,7 @@ def tile_globalprototype_kernel(tc, features, prototypes, out):
                     accum_out=fn2[:, 2 * g + e:2 * g + e + 1],
                 )
 
-        def squares(u, g, pending):
+        def squares(u, g):
             fn2 = norms(u)
             t_ps = state[("t", u, g)]
             halves = t_ps[:].bitcast(BF16).rearrange("m (c e) -> m c e", e=2)
@@ -167,8 +167,6 @@ def tile_globalprototype_kernel(tc, features, prototypes, out):
                     out=junk[:], in_=halves[:, :, e], func=ACT.Square,
                     accum_out=fn2[:, 2 * g + e:2 * g + e + 1],
                 )
-                while pending:
-                    root(pending.pop(0))
 
         def root(u):
             n = 2 * units[u][2] // GROUP
@@ -239,12 +237,18 @@ def tile_globalprototype_kernel(tc, features, prototypes, out):
             rp = state["p"][2]
             r_ps = state[("r", u, c0)]
             w_sb = wp.tile([P, cw], F32, name="w_sb", tag="w_sb")
-            w_view = w_sb[:].rearrange("k (g m e) -> k g m e", m=P, e=2)
-            r_view = r_ps[:].rearrange("k (g e m) -> k g m e", m=P, e=2)
-            if on_scalar:
-                nc.scalar.activation(out=w_view, in_=r_view, func=ACT.Copy, scale=rp[:, 0:1])
-            else:
-                nc.vector.tensor_scalar(out=w_view, in0=r_view, scalar1=rp[:, 0:1], scalar2=None, op0=ALU.mult)
+            pieces = [(0, cw, True)]
+            if u in gram_units and c0 + cw == units[u][2]:
+                pieces = [(0, cw - GROUP, True), (cw - GROUP, cw, False)]
+            for (a, b, paired) in pieces:
+                w_view, r_view = w_sb[:, a:b], r_ps[:, a:b]
+                if paired:
+                    w_view = w_view.rearrange("k (g m e) -> k g m e", m=P, e=2)
+                    r_view = r_view.rearrange("k (g e m) -> k g m e", m=P, e=2)
+                if on_scalar:
+                    nc.scalar.activation(out=w_view, in_=r_view, func=ACT.Copy, scale=rp[:, 0:1])
+                else:
+                    nc.vector.tensor_scalar(out=w_view, in0=r_view, scalar1=rp[:, 0:1], scalar2=None, op0=ALU.mult)
             state[("w", u, c0)] = w_sb
 
         def scale(u, c0, cw):
@@ -305,7 +309,9 @@ def tile_globalprototype_kernel(tc, features, prototypes, out):
                 events[l + ev].append((7.0 + i, "evacuate", u, c0, cw))
                 events[l + sv].append((8.0 + (1 - i if late else i), "scale", u, c0, cw))
 
-        pending = []
+        def norm_last(u):
+            return units[u][2] // GROUP - (2 if u in gram_units else 1)
+
         for s in range(min(AHEAD, n_slots)):
             turn(slots[s][0], slots[s][1])
             if s == 0:
@@ -318,12 +324,9 @@ def tile_globalprototype_kernel(tc, features, prototypes, out):
                 if g == 0 and u + LOADS_AHEAD < n_units:
                     load(u + LOADS_AHEAD)
                 if (u, g) not in gram_slots:
-                    squares(u, g, pending)
-                if s == last[u]:
-                    pending.append(u)
-            else:
-                while pending:
-                    root(pending.pop(0))
+                    squares(u, g)
+                if (u, g) == (u, norm_last(u)):
+                    root(u)
             for (rank, kind, u, c0, cw) in sorted(events[s]):
                 if kind == "regroup":
                     regroup(u)

@@ -24,8 +24,13 @@ GP_COLS = {1024: 416}
 GRAM_UNITS = [6, 8, 10, 12, 14, 16]
 SC_FROM = 3
 EV = 3
+JB = 2
+TAIL_UNITS = 3
+GP_ALL = 0
+TL = 0
+DRANK = 0.7
 SEV = 4
-GP_FROM = 0
+GP_FROM = 4
 CB = 3
 GB = 3
 DG = 1
@@ -59,7 +64,7 @@ def tile_globalprototype_kernel(tc, features, prototypes, out):
         grpp = ctx.enter_context(tc.tile_pool(name="grpp", bufs=GB))
         codp = ctx.enter_context(tc.tile_pool(name="codp", bufs=CB))
         small = ctx.enter_context(tc.tile_pool(name="small", bufs=4))
-        junkp = ctx.enter_context(tc.tile_pool(name="junkp", bufs=2))
+        junkp = ctx.enter_context(tc.tile_pool(name="junkp", bufs=JB))
         wp = ctx.enter_context(tc.tile_pool(name="wp", bufs=4))
         op = ctx.enter_context(tc.tile_pool(name="op", bufs=6))
         tps = ctx.enter_context(tc.psum_pool(name="tps", bufs=4))
@@ -151,7 +156,7 @@ def tile_globalprototype_kernel(tc, features, prototypes, out):
             fn2 = norms(u)
             g_ps = state[("t", u, g)]
             for e in range(2):
-                junk = junkp.tile([P, P], F32, name="gjunk")
+                junk = junkp.tile([P, P], F32, name="gjunk", bufs=2)
                 nc.vector.scalar_tensor_tensor(
                     out=junk[:], in0=g_ps[:, e * P:(e + 1) * P], scalar=1.0, in1=ident_f[:], op0=ALU.mult, op1=ALU.mult,
                     accum_out=fn2[:, 2 * g + e:2 * g + e + 1],
@@ -185,11 +190,14 @@ def tile_globalprototype_kernel(tc, features, prototypes, out):
             raw = raws[u]
             grp = grpp.tile([P, w, PACK], BF16, name="grp", tag="grp", align_bytes=64)
             gp = GP_COLS.get(w, 0) if u >= GP_FROM else 0
+            if u >= n_units - GP_ALL:
+                gp = w
             v = w - gp
-            nc.vector.tensor_copy(
-                out=grp[:, :v, :].rearrange("p (c i) t -> p c t i", i=4),
-                in_=raw[:, :, :v].rearrange("p t (c i) -> p c t i", i=4),
-            )
+            if v:
+                nc.vector.tensor_copy(
+                    out=grp[:, :v, :].rearrange("p (c i) t -> p c t i", i=4),
+                    in_=raw[:, :, :v].rearrange("p t (c i) -> p c t i", i=4),
+                )
             if gp:
                 nc.gpsimd.tensor_scalar(
                     out=grp[:, v:, :], in0=raw[:, :, v:].rearrange("p t c -> p c t"),
@@ -216,9 +224,12 @@ def tile_globalprototype_kernel(tc, features, prototypes, out):
             codes, scales = state[("codes", u)]
             p_codes, p_scales, rp = state["p"]
             for (c0, cw) in chunks(u):
-                d_ps = rps.tile([P, cw], F32, name="x_ps", tag="x_ps")
+                if u >= n_units - TAIL_UNITS:
+                    d_ps = tps.tile([P, PACK * P], F32, name="t_ps")
+                else:
+                    d_ps = rps.tile([P, CHUNK], F32, name="x_ps", tag="x_ps")
                 nc.tensor.matmul_mx(
-                    out=d_ps[:],
+                    out=d_ps[:, :cw],
                     lhsT=p_codes[:].bitcast(FP8X4), lhsT_scale=p_scales[:],
                     rhs=codes[:, c0:c0 + cw].bitcast(FP8X4), rhs_scale=scales[:, c0:c0 + cw],
                     start=True, stop=True,
@@ -258,7 +269,7 @@ def tile_globalprototype_kernel(tc, features, prototypes, out):
             o_sb = state[("o", u)]
             nc.vector.scalar_tensor_tensor(
                 out=o_sb[:, c0:c0 + cw], in0=state[("w", u, c0)][:], scalar=1.0 / EPS,
-                in1=state[("d", u, c0)][:], op0=ALU.min, op1=ALU.mult,
+                in1=state[("d", u, c0)][:, :cw], op0=ALU.min, op1=ALU.mult,
             )
 
         def store(u, c0, cw):
@@ -300,12 +311,13 @@ def tile_globalprototype_kernel(tc, features, prototypes, out):
             events[last[u - RA] + 1 if u >= RA else 0].append((5.0, "regroup", u, 0, 0))
             events[first[u - QA] if u >= QA else 0].append((6.0, "quantise", u, 0, 0))
             events[l + 1].append((0.0, "invert", u, 0, 0))
-            events[l + SPR].append((0.7, "dots", u, 0, 0))
+            events[l + (SPR if u < n_units - TL else 1)].append((DRANK, "dots", u, 0, 0))
             for i, (c0, cw) in enumerate(chunks(u)):
-                events[l + SPR].append((0.6, "spread", u, c0, cw))
+                events[l + (SPR if u < n_units - TL else 1)].append((0.6, "spread", u, c0, cw))
                 late = (u, 512) in SC_CH
-                ev = SEV if (u, c0) in SC_CH else EV
-                sv = SEV if late else EV
+                base_ev = EV if u < n_units - TL else 2
+                ev = SEV if (u, c0) in SC_CH else base_ev
+                sv = SEV if late else base_ev
                 events[l + ev].append((7.0 + i, "evacuate", u, c0, cw))
                 events[l + sv].append((8.0 + (1 - i if late else i), "scale", u, c0, cw))
 

@@ -20,25 +20,25 @@ WIDTHS = [[256, 256, 512, 1024, 1024, 1024], [1024] * 4, [1024] * 4, [1024, 1024
 EPS = 1e-8
 TINY = 2.0 ** -116
 S_EVAC = [1, 0]
-GP_COLS = {1024: 416}
-GRAM_UNITS = [6, 8, 10, 12, 14, 16]
+GP_COLS = {1024: 384}
+GRAM_UNITS = [5, 7, 9, 11, 13, 15]
 SC_FROM = 3
 EV = 3
-JB = 2
+JB = 12
 TAIL_UNITS = 3
-GP_ALL = 0
+GP_ALL = 2
 TL = 0
 DRANK = 0.7
 SEV = 4
-GP_FROM = 4
+GP_FROM = 5
 CB = 3
-GB = 3
+GB = 2
 DG = 1
 GA = 2
 RA = 2
 QA = 0
 SPR = 2
-SC_CH = [(u, 512) for u in range(4, 17, 2)]
+SC_CH = [(u, 512) for u in range(3, 17, 2)]
 MANUAL = True
 
 FLOPS = 2 * B * HW * C * K
@@ -309,7 +309,7 @@ def tile_globalprototype_kernel(tc, features, prototypes, out):
                 events[f - GA].append((9.6, "gram", u, 0, 0))
                 events[f - GA + DG].append((9.5, "diagonals", u, 0, 0))
             events[last[u - RA] + 1 if u >= RA else 0].append((5.0, "regroup", u, 0, 0))
-            events[first[u - QA] if u >= QA else 0].append((6.0, "quantise", u, 0, 0))
+            events[first[u - QA] if u >= QA else 0].append((4.5 if u >= 2 else 6.0, "quantise", u, 0, 0))
             events[l + 1].append((0.0, "invert", u, 0, 0))
             events[l + (SPR if u < n_units - TL else 1)].append((DRANK, "dots", u, 0, 0))
             for i, (c0, cw) in enumerate(chunks(u)):

from contextlib import ExitStack

import concourse.mybir as mybir
from concourse.masks import make_identity

F32 = mybir.dt.float32
BF16 = mybir.dt.bfloat16
U32 = mybir.dt.uint32
U8 = mybir.dt.uint8
FP8X4 = mybir.dt.float8_e4m3fn_x4
ACT = mybir.ActivationFunctionType
ALU = mybir.AluOpType

P = 128
PACK = 4
B, C, HW, K = 4, 512, 4096, 128
CHUNK = 512
GROUP = 256
WIDTHS = [[256, 256, 512, 1024, 1024, 1024], [1024] * 4, [1024] * 4, [1024, 1024, 1024, 512, 256, 256]]
EPS = 1e-8
TINY = 2.0 ** -116
S_EVAC = [1, 0]
GP_COLS = {1024: 384}
GRAM_UNITS = [5, 7, 9, 11, 13, 15]
SC_FROM = 3
EV = 3
JB = 12
TAIL_UNITS = 3
GP_ALL = 2
TL = 0
DRANK = 0.7
SEV = 4
GP_FROM = 5
CB = 3
GB = 2
DG = 1
GA = 2
RA = 2
QA = 0
SPR = 2
SC_CH = [(u, 512) for u in range(3, 17, 2)]
MANUAL = True

FLOPS = 2 * B * HW * C * K


def tile_globalprototype_kernel(tc, features, prototypes, out):
    nc = tc.nc
    units = []
    for b in range(B):
        off = 0
        for w in WIDTHS[b]:
            units.append((b, off, w))
            off += w
        assert off == HW
    n_units = len(units)
    count = {}
    for (b, off, w) in units:
        count[w] = count.get(w, 0) + 1

    with ExitStack() as ctx:
        const = ctx.enter_context(tc.tile_pool(name="const", bufs=1))
        rawp = ctx.enter_context(tc.tile_pool(name="rawp", bufs=1))
        grpp = ctx.enter_context(tc.tile_pool(name="grpp", bufs=GB))
        codp = ctx.enter_context(tc.tile_pool(name="codp", bufs=CB))
        small = ctx.enter_context(tc.tile_pool(name="small", bufs=4))
        junkp = ctx.enter_context(tc.tile_pool(name="junkp", bufs=JB))
        wp = ctx.enter_context(tc.tile_pool(name="wp", bufs=4))
        op = ctx.enter_context(tc.tile_pool(name="op", bufs=6))
        tps = ctx.enter_context(tc.psum_pool(name="tps", bufs=4))
        rps = ctx.enter_context(tc.psum_pool(name="rps", bufs=4))
        if MANUAL:
            ctx.enter_context(tc.manual_schedule())

        raws = []

        def load(u):
            b, off, w = units[u]
            raw = rawp.tile([P, PACK, w], BF16, name="raw%d" % w, tag="raw%d" % w, bufs=count[w])
            src = features[b].rearrange("(p j) h w -> p j (h w)", j=PACK)
            nc.sync.dma_start(out=raw[:], in_=src[:, :, off:off + w])
            raws.append(raw)

        p_sb = const.tile([P, C], BF16)
        LOADS_AHEAD = 7
        load(0)
        nc.sync.dma_start(out=p_sb[:], in_=prototypes)
        for u in range(1, LOADS_AHEAD):
            load(u)

        tiny = const.tile([P, 1], F32)
        nc.vector.memset(tiny[:], TINY)
        warm = const.tile([P, 1], F32)
        nc.scalar.activation(out=warm[:], in_=tiny[:], func=ACT.Sqrt, bias=tiny[:, 0:1])
        ident_f = const.tile([P, P], F32)
        make_identity(nc, ident_f[:])
        ident_b = const.tile([P, P], BF16)
        make_identity(nc, ident_b[:])

        state = {}

        def prototypes_turn():
            p_t = const.tile([P, PACK, P], BF16)
            nc.vector.tensor_copy(out=p_t[:], in_=p_sb[:].rearrange("k (p t) -> k t p", t=PACK))
            p_ps = rps.tile([P, PACK, P], BF16, name="x_ps", tag="x_ps")
            for t in range(PACK):
                nc.tensor.transpose(p_ps[:, t, :], p_t[:, t, :], ident_b[:])
            state["p_ps"] = p_ps

        def prototypes_finish():
            pjunk = junkp.tile([P, C], BF16, name="junk")
            pn2 = const.tile([P, 1], F32)
            nc.scalar.activation(out=pjunk[:], in_=p_sb[:], func=ACT.Square, accum_out=pn2[:])
            pn = const.tile([P, 1], F32)
            nc.scalar.activation(out=pn[:], in_=pn2[:], func=ACT.Sqrt, bias=tiny[:, 0:1])
            p_grp = const.tile([P, K, PACK], BF16, align_bytes=64)
            nc.vector.tensor_copy(out=p_grp[:], in_=state["p_ps"][:].rearrange("p t k -> p k t"))
            rp = const.tile([P, 1], F32)
            nc.vector.reciprocal(out=rp[:], in_=pn[:])
            p_codes = const.tile([P, K], U32, align_bytes=64)
            p_scales = const.tile([P, K], U8, align_bytes=64)
            nc.vector.quantize_mx(
                out=p_codes[:].bitcast(FP8X4),
                scales=p_scales[:],
                in_=p_grp[:].rearrange("p k t -> p (k t)"),
            )
            state["p"] = (p_codes, p_scales, rp)

        def transposes(u, g):
            raw = raws[u]
            t_ps = tps.tile([P, PACK * P], F32, name="t_ps")
            for t in range(PACK):
                words = raw[:, t, :].bitcast(F32)
                nc.tensor.transpose(t_ps[:, t * P:(t + 1) * P], words[:, g * P:(g + 1) * P], ident_f[:])
            state[("t", u, g)] = t_ps

        def gram(u, g):
            raw = raws[u]
            g_ps = rps.tile([P, 2 * P], F32, name="x_ps", tag="x_ps")
            for e in range(2):
                cols = slice(g * GROUP + e * P, g * GROUP + (e + 1) * P)
                for t in range(PACK):
                    nc.tensor.matmul(
                        g_ps[:, e * P:(e + 1) * P], lhsT=raw[:, t, cols], rhs=raw[:, t, cols],
                        start=(t == 0), stop=(t == PACK - 1),
                    )
            state[("t", u, g)] = g_ps

        def norms(u):
            if ("fn2", u) not in state:
                fn2_new = small.tile([P, 8], F32, name="fn2")
                state[("fn2", u)] = fn2_new
            return state[("fn2", u)]

        def diagonals(u, g):
            fn2 = norms(u)
            g_ps = state[("t", u, g)]
            for e in range(2):
                junk = junkp.tile([P, P], F32, name="gjunk", bufs=2)
                nc.vector.scalar_tensor_tensor(
                    out=junk[:], in0=g_ps[:, e * P:(e + 1) * P], scalar=1.0, in1=ident_f[:], op0=ALU.mult, op1=ALU.mult,
                    accum_out=fn2[:, 2 * g + e:2 * g + e + 1],
                )

        def squares(u, g):
            fn2 = norms(u)
            t_ps = state[("t", u, g)]
            halves = t_ps[:].bitcast(BF16).rearrange("m (c e) -> m c e", e=2)
            for e in range(2):
                junk = junkp.tile([P, C], BF16, name="junk")
                nc.scalar.activation(
                    out=junk[:], in_=halves[:, :, e], func=ACT.Square,
                    accum_out=fn2[:, 2 * g + e:2 * g + e + 1],
                )

        def root(u):
            n = 2 * units[u][2] // GROUP
            fn = small.tile([P, 8], F32, name="fn")
            nc.scalar.activation(out=fn[:, :n], in_=state[("fn2", u)][:, :n], func=ACT.Sqrt, bias=tiny[:, 0:1])
            state[("fn", u)] = fn

        def invert(u):
            n = 2 * units[u][2] // GROUP
            rf = small.tile([P, 8], F32, name="rf")
            nc.vector.reciprocal(out=rf[:, :n], in_=state[("fn", u)][:, :n])
            state[("rf", u)] = rf

        def regroup(u):
            w = units[u][2]
            raw = raws[u]
            grp = grpp.tile([P, w, PACK], BF16, name="grp", tag="grp", align_bytes=64)
            gp = GP_COLS.get(w, 0) if u >= GP_FROM else 0
            if u >= n_units - GP_ALL:
                gp = w
            v = w - gp
            if v:
                nc.vector.tensor_copy(
                    out=grp[:, :v, :].rearrange("p (c i) t -> p c t i", i=4),
                    in_=raw[:, :, :v].rearrange("p t (c i) -> p c t i", i=4),
                )
            if gp:
                nc.gpsimd.tensor_scalar(
                    out=grp[:, v:, :], in0=raw[:, :, v:].rearrange("p t c -> p c t"),
                    scalar1=1.0, scalar2=0.0, op0=ALU.mult, op1=ALU.add,
                )
            state[("grp", u)] = grp

        def quantise(u):
            w = units[u][2]
            grp = state[("grp", u)]
            codes = codp.tile([P, w], U32, name="codes", tag="codes", align_bytes=64)
            scales = codp.tile([P, w], U8, name="scales", tag="scales", align_bytes=64)
            nc.vector.quantize_mx(
                out=codes[:].bitcast(FP8X4), scales=scales[:], in_=grp[:].rearrange("p w t -> p (w t)"),
            )
            state[("codes", u)] = (codes, scales)

        def chunks(u):
            w = units[u][2]
            cw = min(w, CHUNK)
            return [(c * cw, cw) for c in range(w // cw)]

        def dots(u):
            codes, scales = state[("codes", u)]
            p_codes, p_scales, rp = state["p"]
            for (c0, cw) in chunks(u):
                if u >= n_units - TAIL_UNITS:
                    d_ps = tps.tile([P, PACK * P], F32, name="t_ps")
                else:
                    d_ps = rps.tile([P, CHUNK], F32, name="x_ps", tag="x_ps")
                nc.tensor.matmul_mx(
                    out=d_ps[:, :cw],
                    lhsT=p_codes[:].bitcast(FP8X4), lhsT_scale=p_scales[:],
                    rhs=codes[:, c0:c0 + cw].bitcast(FP8X4), rhs_scale=scales[:, c0:c0 + cw],
                    start=True, stop=True,
                )
                state[("d", u, c0)] = d_ps

        def spread(u, c0, cw):
            rf = state[("rf", u)]
            r_ps = rps.tile([P, cw], F32, name="x_ps", tag="x_ps")
            for i in range(cw // P):
                col = c0 // P + i
                nc.tensor.transpose(r_ps[:, i * P:(i + 1) * P], rf[:, col:col + 1].to_broadcast([P, P]), ident_f[:])
            state[("r", u, c0)] = r_ps

        def evacuate(u, c0, cw, on_scalar):
            rp = state["p"][2]
            r_ps = state[("r", u, c0)]
            w_sb = wp.tile([P, cw], F32, name="w_sb", tag="w_sb")
            pieces = [(0, cw, True)]
            if u in gram_units and c0 + cw == units[u][2]:
                pieces = [(0, cw - GROUP, True), (cw - GROUP, cw, False)]
            for (a, b, paired) in pieces:
                w_view, r_view = w_sb[:, a:b], r_ps[:, a:b]
                if paired:
                    w_view = w_view.rearrange("k (g m e) -> k g m e", m=P, e=2)
                    r_view = r_view.rearrange("k (g e m) -> k g m e", m=P, e=2)
                if on_scalar:
                    nc.scalar.activation(out=w_view, in_=r_view, func=ACT.Copy, scale=rp[:, 0:1])
                else:
                    nc.vector.tensor_scalar(out=w_view, in0=r_view, scalar1=rp[:, 0:1], scalar2=None, op0=ALU.mult)
            state[("w", u, c0)] = w_sb

        def scale(u, c0, cw):
            if ("o", u) not in state:
                o_new = op.tile([P, units[u][2]], F32, name="o_sb", tag="o_sb")
                state[("o", u)] = o_new
            o_sb = state[("o", u)]
            nc.vector.scalar_tensor_tensor(
                out=o_sb[:, c0:c0 + cw], in0=state[("w", u, c0)][:], scalar=1.0 / EPS,
                in1=state[("d", u, c0)][:, :cw], op0=ALU.min, op1=ALU.mult,
            )

        def store(u, c0, cw):
            b, off, w = units[u]
            dst = out[b].rearrange("k h w -> k (h w)")
            nc.sync.dma_start(out=dst[:, off + c0:off + c0 + cw], in_=state[("o", u)][:, c0:c0 + cw])

        n_evac = [0]

        def on_scalar():
            n_evac[0] += 1
            return S_EVAC[n_evac[0] % len(S_EVAC)] == 1

        slots = []
        first = {}
        last = {}
        for u in range(n_units):
            for g in range(units[u][2] // GROUP):
                if g == 0:
                    first[u] = len(slots)
                last[u] = len(slots)
                slots.append((u, g))
        n_slots = len(slots)
        gram_units = GRAM_UNITS
        gram_slots = [(u, units[u][2] // GROUP - 1) for u in gram_units]

        def turn(u, g):
            if (u, g) not in gram_slots:
                transposes(u, g)

        AHEAD = 3
        TAIL = 16
        events = [[] for s in range(n_slots + TAIL)]
        for u in range(n_units):
            f, l = first[u], last[u]
            if u in gram_units:
                events[f - GA].append((9.6, "gram", u, 0, 0))
                events[f - GA + DG].append((9.5, "diagonals", u, 0, 0))
            events[last[u - RA] + 1 if u >= RA else 0].append((5.0, "regroup", u, 0, 0))
            events[first[u - QA] if u >= QA else 0].append((4.5 if u >= 2 else 6.0, "quantise", u, 0, 0))
            events[l + 1].append((0.0, "invert", u, 0, 0))
            events[l + (SPR if u < n_units - TL else 1)].append((DRANK, "dots", u, 0, 0))
            for i, (c0, cw) in enumerate(chunks(u)):
                events[l + (SPR if u < n_units - TL else 1)].append((0.6, "spread", u, c0, cw))
                late = (u, 512) in SC_CH
                base_ev = EV if u < n_units - TL else 2
                ev = SEV if (u, c0) in SC_CH else base_ev
                sv = SEV if late else base_ev
                events[l + ev].append((7.0 + i, "evacuate", u, c0, cw))
                events[l + sv].append((8.0 + (1 - i if late else i), "scale", u, c0, cw))

        def norm_last(u):
            return units[u][2] // GROUP - (2 if u in gram_units else 1)

        for s in range(min(AHEAD, n_slots)):
            turn(slots[s][0], slots[s][1])
            if s == 0:
                prototypes_turn()
        for s in range(n_slots + TAIL):
            if s + AHEAD < n_slots:
                turn(slots[s + AHEAD][0], slots[s + AHEAD][1])
            if s < n_slots:
                u, g = slots[s]
                if g == 0 and u + LOADS_AHEAD < n_units:
                    load(u + LOADS_AHEAD)
                if (u, g) not in gram_slots:
                    squares(u, g)
                if (u, g) == (u, norm_last(u)):
                    root(u)
            for (rank, kind, u, c0, cw) in sorted(events[s]):
                if kind == "regroup":
                    regroup(u)
                elif kind == "gram":
                    gram(u, units[u][2] // GROUP - 1)
                elif kind == "diagonals":
                    diagonals(u, units[u][2] // GROUP - 1)
                elif kind == "quantise":
                    quantise(u)
                elif kind == "invert":
                    invert(u)
                elif kind == "dots":
                    dots(u)
                elif kind == "spread":
                    spread(u, c0, cw)
                elif kind == "evacuate":
                    evacuate(u, c0, cw, ((u, c0) in SC_CH) or u >= n_units - SC_FROM)
                else:
                    scale(u, c0, cw)
                    store(u, c0, cw)
            if s == 0:
                prototypes_finish()
